import numpy as np
import ml_dtypes


BF16 = ml_dtypes.bfloat16


def bf(x):
    return np.asarray(x, np.float32).astype(BF16)


def f64(x):
    return np.asarray(x).astype(np.float64)


E2M1 = np.array([0.0, 0.5, 1.0, 1.5, 2.0, 3.0, 4.0, 6.0, -0.0, -0.5, -1.0, -1.5, -2.0, -3.0, -4.0, -6.0])


def pack_weight(w, fmt):
    k, n = w.shape
    w = f64(bf(w)).reshape(k // 32, 32, n)
    amax = np.abs(w).max(1)
    if fmt == "e4m3":
        byte = np.frexp(amax)[1] - 1 + 127 - 7
    else:
        mant, ex = np.frexp(amax / 6.0)
        byte = np.where(mant > 0.5, ex, ex - 1) + 127
    byte = np.clip(np.where(amax > 0, byte, 1), 1, 254)
    scaled = (w * np.exp2(127.0 - byte)[:, None, :]).reshape(k, n).astype(np.float32)
    by_word = np.ascontiguousarray(scaled.reshape(k // 512, 128, 4, n).transpose(0, 1, 3, 2))
    if fmt == "e4m3":
        words = by_word.astype(ml_dtypes.float8_e4m3fn).view(np.uint8)
    else:
        c = by_word.astype(ml_dtypes.float4_e2m1fn).view(np.uint8) & 0xF
        words = c[..., 0::2] | (c[..., 1::2] << 4)
    return np.ascontiguousarray(words), np.ascontiguousarray(byte.astype(np.uint8).reshape(k // 512, 16, n))


def unpack_weight(words, scales, fmt):
    g, p, n, _ = words.shape
    if fmt == "e4m3":
        vals = np.ascontiguousarray(words).view(ml_dtypes.float8_e4m3fn).astype(np.float64)
    else:
        nib = np.empty((g, p, n, 4), np.uint8)
        nib[..., 0::2] = words & 0xF
        nib[..., 1::2] = words >> 4
        vals = E2M1[nib]
    vals = vals * np.repeat(np.exp2(scales.astype(np.float64) - 127.0), 8, axis=1)[..., None]
    return vals.transpose(0, 1, 3, 2).reshape(g * 512, n)

def pack4(w):
    words, scales = pack_weight(w, "e2m1")
    return words.reshape(words.shape[0], 128, -1), scales


def unpack4(words, scales):
    return unpack_weight(words.reshape(words.shape[0], 128, -1, 2), scales, "e2m1")


def kspread(k):
    return np.exp2(np.repeat(np.random.randint(-6, 7, k // 32), 32).astype(np.float64))


B, S, T, E, D, H = 1, 1024, 1024, 4096, 4096, 16
DK = D // H


def rope_tables(n):
    m = np.arange(n, dtype=np.float64)[:, None]
    i = np.repeat(np.arange(DK // 2, dtype=np.float64), 2)[None, :]
    ang = m * np.exp(-(2.0 * np.log(1e4) / DK) * i)
    return np.cos(ang), np.sin(ang)


def rotate_pairs(x):
    return np.stack([-x[..., 1::2], x[..., 0::2]], axis=-1).reshape(x.shape)


def setup_inputs():
    s = kspread(E)
    x = np.random.standard_normal((B, S, E)) * s
    x_words, x_scales = pack4(x.reshape(B * S, E).T)
    w_words, w_scales = pack4(np.random.standard_normal((E, D)) * 1.1 / np.sqrt(E) / s[:, None])
    b = bf(np.random.standard_normal(D) * 0.4)
    return {"x_words": x_words, "x_scales": x_scales, "w_words": w_words, "w_scales": w_scales, "b": b}


def reference(x_words, x_scales, w_words, w_scales, b):
    p = (unpack4(x_words, x_scales).T.reshape(B, S, E) @ unpack4(w_words, w_scales)) + f64(b)
    p = p.reshape(B, S, H, DK).transpose(0, 2, 1, 3)
    r1, r2 = rope_tables(S)
    return p * r1 + rotate_pairs(p) * r2

@@ -1,0 +1,276 @@
+from contextlib import ExitStack
+
+import concourse.mybir as mybir
+
+F32 = mybir.dt.float32
+BF16 = mybir.dt.bfloat16
+I32 = mybir.dt.int32
+U8 = mybir.dt.uint8
+FP4X4 = mybir.dt.float4_e2m1fn_x4
+ALU = mybir.AluOpType
+FUNC = mybir.ActivationFunctionType
+
+P = 128
+G = 8
+TB = 8
+NB = 8
+NW = 512
+DK = 256
+HALF = DK // 2
+FLOPS = 2 * 1024 * 4096 * 4096
+
+PI = 3.141592653589793
+G_COLS = 128
+WARM = 5
+
+
+def tile_multiheadedattention_pa_kernel(tc, x_words, x_scales, w_words, w_scales, b, out):
+    nc = tc.nc
+    with ExitStack() as ctx:
+        keep = ctx.enter_context(tc.tile_pool(name="keep", bufs=1))
+        work = ctx.enter_context(tc.tile_pool(name="work", bufs=3))
+        outp = ctx.enter_context(tc.tile_pool(name="outp", bufs=6))
+        psum = ctx.enter_context(tc.psum_pool(name="psum", bufs=8))
+        ctx.enter_context(tc.manual_schedule())
+
+        x_codes = {}
+        x_scale = {}
+        w_codes = {}
+        w_scale = {}
+
+        def x_code_tile(name, g0, g1, tb0, tb1):
+            t = keep.tile([P, g1 - g0, 256 * (tb1 - tb0)], U8, name=name, align_bytes=64)
+            for g in range(g0, g1):
+                for tb in range(tb0, tb1):
+                    x_codes[(tb, g)] = t[:, g - g0, 256 * (tb - tb0) : 256 * (tb - tb0 + 1)]
+            return t
+
+        def x_plane_tile(name, tb0, tb1):
+            t = keep.tile([P, G, P * (tb1 - tb0)], U8, name=name, align_bytes=64)
+            for g in range(G):
+                for tb in range(tb0, tb1):
+                    x_scale[(tb, g)] = t[:, g, P * (tb - tb0) : P * (tb - tb0 + 1)]
+            return t
+
+        def w_code_tile(name, nb, g0, g1):
+            t = keep.tile([P, g1 - g0, 2 * NW], U8, name=name, align_bytes=64)
+            for g in range(g0, g1):
+                w_codes[(nb, g)] = t[:, g - g0, :]
+            return t
+
+        def w_plane_tile(name, nb):
+            t = keep.tile([P, G, NW], U8, name=name, align_bytes=64)
+            for g in range(G):
+                w_scale[(nb, g)] = t[:, g, :]
+            return t
+
+        def load_codes(dst, words, g0, g1, byte0, byte1):
+            nc.sync.dma_start(
+                out=dst[:].bitcast(I32),
+                in_=words[g0:g1, :, byte0:byte1].rearrange("g p n -> p g n").bitcast(I32),
+            )
+
+        def load_scales(dst, scales, col0, col1):
+            for q in range(4):
+                nc.sync.dma_start(
+                    out=dst[32 * q : 32 * q + 4, :, :].bitcast(I32),
+                    in_=scales[:, 4 * q : 4 * q + 4, col0:col1].rearrange("g r n -> r g n").bitcast(I32),
+                )
+
+        xc01a = x_code_tile("xc01a", 0, 4, 0, 2)
+        xc01b = x_code_tile("xc01b", 4, 8, 0, 2)
+        xc23 = x_code_tile("xc23", 0, 8, 2, 4)
+        xc47a = x_code_tile("xc47a", 0, 4, 4, 8)
+        xc47b = x_code_tile("xc47b", 4, 8, 4, 8)
+        xs01 = x_plane_tile("xs01", 0, 2)
+        xs23 = x_plane_tile("xs23", 2, 4)
+        xs47 = x_plane_tile("xs47", 4, 8)
+        wc0a = w_code_tile("wc0a", 0, 0, 2)
+        wc0b = w_code_tile("wc0b", 0, 2, 5)
+        wc0c = w_code_tile("wc0c", 0, 5, 8)
+        wcs = [None] + [w_code_tile("wc%d" % nb, nb, 0, G) for nb in range(1, NB)]
+        wss = [w_plane_tile("ws%d" % nb, nb) for nb in range(NB)]
+        bias0 = keep.tile([P, NW], BF16, name="bias0")
+        bias1 = keep.tile([P, (NB - 1) * NW], BF16, name="bias1")
+
+        def zero_v(plane):
+            nc.vector.memset(plane[:].bitcast(I32), 0)
+
+        def zero_g(plane):
+            nc.gpsimd.memset(plane[:].bitcast(F32), 0.0)
+
+        ones = keep.tile([P, 1], F32, name="ones")
+        nc.vector.memset(ones[:], 1.0)
+        zero_v(xs01)
+        zero_v(wss[0])
+        zero_v(xs23)
+
+        pos = keep.tile([P, TB], F32, name="pos")
+        nc.gpsimd.iota(pos[:], pattern=[[P, TB]], base=0, channel_multiplier=1, allow_small_or_imprecise_dtypes=True)
+        cold = keep.tile([P, P + NW], BF16, name="cold")
+        nc.gpsimd.memset(cold[:], 0.0)
+
+        junk = keep.tile([P, 1], F32, name="junk")
+        nc.scalar.activation(out=junk[:], in_=ones[:], func=FUNC.Sin)
+
+        load_codes(wc0a, w_words, 0, 2, 0, 2 * NW)
+        load_codes(xc01a, x_words, 0, 4, 0, 512)
+        load_scales(xs01, x_scales, 0, 256)
+        load_scales(wss[0], w_scales, 0, NW)
+        load_codes(wc0b, w_words, 2, 5, 0, 2 * NW)
+        load_codes(xc01b, x_words, 4, 8, 0, 512)
+        load_codes(wc0c, w_words, 5, 8, 0, 2 * NW)
+        nc.sync.dma_start(out=bias0[:], in_=b[0:NW].partition_broadcast(P))
+        load_scales(xs23, x_scales, 256, 512)
+        load_codes(xc23, x_words, 0, 8, 512, 1024)
+
+        for i in range(WARM):
+            dummy = psum.tile([P, NW], F32, name="acc")
+            nc.tensor.matmul(out=dummy[:], lhsT=cold[:, 0:P], rhs=cold[:, P : P + NW], start=True, stop=True)
+
+        turns = keep.tile([P, HALF], F32, name="turns")
+        for j in range(4):
+            nc.vector.tensor_scalar(
+                out=turns[:, j : j + 1], in0=ones[:], scalar1=10.0 ** (-j / 32.0) / (2.0 * PI), scalar2=None, op0=ALU.mult
+            )
+        for w in (4, 16):
+            for m in range(1, 4):
+                nc.vector.tensor_scalar(
+                    out=turns[:, w * m : w * (m + 1)], in0=turns[:, 0:w], scalar1=10.0 ** (-w * m / 32.0), scalar2=None, op0=ALU.mult
+                )
+        nc.vector.tensor_scalar(out=turns[:, 64:128], in0=turns[:, 0:64], scalar1=10.0 ** (-2.0), scalar2=None, op0=ALU.mult)
+        halfpi = keep.tile([P, 1], F32, name="halfpi")
+        nc.vector.tensor_scalar(out=halfpi[:], in0=ones[:], scalar1=PI / 2.0, scalar2=None, op0=ALU.mult)
+
+        frac = {}
+
+        def reduce_angles(name, tb0, tb1):
+            n = tb1 - tb0
+            u = keep.tile([P, n, HALF], F32, name="u" + name)
+            k = keep.tile([P, n, HALF], I32, name="k" + name)
+            d = keep.tile([P, n, HALF], F32, name="d" + name)
+            for tb in range(tb0, tb1):
+                nc.vector.tensor_scalar(out=u[:, tb - tb0, :], in0=turns[:], scalar1=pos[:, tb : tb + 1], scalar2=None, op0=ALU.mult)
+            nc.vector.tensor_copy(out=k[:], in_=u[:])
+            nc.vector.tensor_tensor(out=d[:], in0=u[:], in1=k[:], op=ALU.subtract)
+            for tb in range(tb0, tb1):
+                frac[tb] = d[:, tb - tb0, :]
+
+        reduce_angles("a", 0, 2)
+        reduce_angles("b", 2, 8)
+        zero_v(xs47)
+        zero_v(wss[1])
+        zero_v(wss[2])
+
+        load_scales(xs47, x_scales, 512, 1024)
+        load_codes(xc47a, x_words, 0, 4, 1024, 2048)
+        load_codes(xc47b, x_words, 4, 8, 1024, 2048)
+        load_scales(wss[1], w_scales, NW, 2 * NW)
+        load_codes(wcs[1], w_words, 0, G, 2 * NW, 4 * NW)
+        nc.sync.dma_start(out=bias1[:], in_=b[NW : NB * NW].partition_broadcast(P))
+        load_scales(wss[2], w_scales, 2 * NW, 3 * NW)
+        load_codes(wcs[2], w_words, 0, G, 4 * NW, 6 * NW)
+
+        cos2 = {}
+        sin2 = {}
+
+        def tables(tb):
+            c = keep.tile([P, DK], F32, name="cos%d" % tb)
+            s = keep.tile([P, DK], F32, name="sin%d" % tb)
+            mag = work.tile([P, HALF], F32, name="mag")
+            s3 = s[:].rearrange("p (i e) -> p i e", e=2)
+            nc.scalar.activation(out=mag[:], in_=frac[tb], func=FUNC.Abs)
+            nc.scalar.activation(out=s3[:, :, 0], in_=frac[tb], func=FUNC.Sin, scale=-2.0 * PI)
+            nc.scalar.activation(out=s3[:, :, 1], in_=frac[tb], func=FUNC.Sin, scale=2.0 * PI)
+            nc.scalar.activation(
+                out=c[:].rearrange("p (i e) -> p i e", e=2),
+                in_=mag[:].unsqueeze(2).to_broadcast([P, HALF, 2]),
+                func=FUNC.Sin,
+                scale=-2.0 * PI,
+                bias=halfpi[:, 0:1],
+            )
+            cos2[tb] = c
+            sin2[tb] = s
+
+        for tb in range(3):
+            tables(tb)
+
+        order = [(nb, tb) for nb in range(NB) for tb in range(TB)]
+        acc = {}
+        zt = {}
+        at = {}
+        tt = {}
+
+        def mx_pass(k, g):
+            nb, tb = order[k]
+            nc.tensor.matmul_mx(
+                out=acc[k][:],
+                lhsT=x_codes[(tb, g)].bitcast(FP4X4),
+                lhsT_scale=x_scale[(tb, g)],
+                rhs=w_codes[(nb, g)].bitcast(FP4X4),
+                rhs_scale=w_scale[(nb, g)],
+                start=(g == 0),
+                stop=(g == G - 1),
+            )
+
+        def add_bias(k):
+            nb, tb = order[k]
+            z = work.tile([P, NW], F32, name="z")
+            bias = bias0[:] if nb == 0 else bias1[:, (nb - 1) * NW : nb * NW]
+            nc.vector.tensor_tensor(out=z[:], in0=acc[k][:], in1=bias, op=ALU.add)
+            zt[k] = z
+
+        def products(k):
+            nb, tb = order[k]
+            z = zt[k]
+            a = work.tile([P, NW], F32, name="a")
+            t = work.tile([P, NW], F32, name="t")
+            nc.vector.tensor_tensor(
+                out=a[:].rearrange("p (h c) -> p h c", h=2),
+                in0=z[:].rearrange("p (h c) -> p h c", h=2),
+                in1=cos2[tb][:].unsqueeze(1).to_broadcast([P, 2, DK]),
+                op=ALU.mult,
+            )
+            nc.vector.tensor_tensor(
+                out=t[:].rearrange("p (h i e) -> p h i e", h=2, e=2),
+                in0=z[:].rearrange("p (h i e) -> p h i e", h=2, e=2)[:, :, :, ::-1],
+                in1=sin2[tb][:].rearrange("p (i e) -> p i e", e=2).unsqueeze(1).to_broadcast([P, 2, HALF, 2]),
+                op=ALU.mult,
+            )
+            at[k] = a
+            tt[k] = t
+
+        def finish(k):
+            nb, tb = order[k]
+            o = outp.tile([P, NW], F32, name="o")
+            nc.gpsimd.tensor_tensor(out=o[:, 0:G_COLS], in0=at[k][:, 0:G_COLS], in1=tt[k][:, 0:G_COLS], op=ALU.add)
+            nc.vector.tensor_tensor(out=o[:, G_COLS:NW], in0=at[k][:, G_COLS:NW], in1=tt[k][:, G_COLS:NW], op=ALU.add)
+            nc.scalar.dma_start(
+                out=out[0, 2 * nb : 2 * nb + 2, P * tb : P * (tb + 1), :].rearrange("h p j -> p h j"),
+                in_=o[:].rearrange("p (h j) -> p h j", h=2),
+            )
+
+        for k in range(len(order)):
+            if k == 0:
+                acc[0] = psum.tile([P, NW], F32, name="acc")
+                acc[1] = psum.tile([P, NW], F32, name="acc")
+                for gs in ((0, 1), (2, 3), (4,), (5, 6, 7)):
+                    for kk in (0, 1):
+                        for g in gs:
+                            mx_pass(kk, g)
+            elif k > 1:
+                acc[k] = psum.tile([P, NW], F32, name="acc")
+                for g in range(G):
+                    mx_pass(k, g)
+            if k + 3 < TB:
+                tables(k + 3)
+            add_bias(k)
+            if k >= 1:
+                finish(k - 1)
+            if 1 <= k <= NB - 3:
+                nb = k + 2
+                zero_g(wss[nb])
+                load_scales(wss[nb], w_scales, nb * NW, (nb + 1) * NW)
+                load_codes(wcs[nb], w_words, 0, G, 2 * nb * NW, 2 * (nb + 1) * NW)
+            products(k)
+        finish(len(order) - 1)

@@ -21,7 +21,7 @@ FLOPS = 2 * 1024 * 4096 * 4096
 
 PI = 3.141592653589793
 G_COLS = 128
-WARM = 5
+WARM = 6
 
 
 def tile_multiheadedattention_pa_kernel(tc, x_words, x_scales, w_words, w_scales, b, out):
@@ -99,19 +99,20 @@ def tile_multiheadedattention_pa_kernel(tc, x_words, x_scales, w_words, w_scales
         def zero_g(plane):
             nc.gpsimd.memset(plane[:].bitcast(F32), 0.0)
 
-        ones = keep.tile([P, 1], F32, name="ones")
-        nc.vector.memset(ones[:], 1.0)
+        ones = keep.tile([P, 2], F32, name="ones")
+        nc.vector.memset(ones[:, 0:1], 1.0)
+        nc.vector.memset(ones[:, 1:2], -1.0)
         zero_v(xs01)
         zero_v(wss[0])
+        cold = keep.tile([P, P + NW], BF16, name="cold")
+        nc.vector.memset(cold[:], 0.0)
         zero_v(xs23)
 
         pos = keep.tile([P, TB], F32, name="pos")
         nc.gpsimd.iota(pos[:], pattern=[[P, TB]], base=0, channel_multiplier=1, allow_small_or_imprecise_dtypes=True)
-        cold = keep.tile([P, P + NW], BF16, name="cold")
-        nc.gpsimd.memset(cold[:], 0.0)
 
         junk = keep.tile([P, 1], F32, name="junk")
-        nc.scalar.activation(out=junk[:], in_=ones[:], func=FUNC.Sin)
+        nc.scalar.activation(out=junk[:], in_=ones[:, 0:1], func=FUNC.Sin)
 
         load_codes(wc0a, w_words, 0, 2, 0, 2 * NW)
         load_codes(xc01a, x_words, 0, 4, 0, 512)
@@ -128,27 +129,27 @@ def tile_multiheadedattention_pa_kernel(tc, x_words, x_scales, w_words, w_scales
             dummy = psum.tile([P, NW], F32, name="acc")
             nc.tensor.matmul(out=dummy[:], lhsT=cold[:, 0:P], rhs=cold[:, P : P + NW], start=True, stop=True)
 
-        turns = keep.tile([P, HALF], F32, name="turns")
+        turns = keep.tile([P, DK], F32, name="turns")
         for j in range(4):
             nc.vector.tensor_scalar(
-                out=turns[:, j : j + 1], in0=ones[:], scalar1=10.0 ** (-j / 32.0) / (2.0 * PI), scalar2=None, op0=ALU.mult
+                out=turns[:, 2 * j : 2 * j + 2], in0=ones[:], scalar1=10.0 ** (-j / 32.0) / (2.0 * PI), scalar2=None, op0=ALU.mult
             )
         for w in (4, 16):
             for m in range(1, 4):
                 nc.vector.tensor_scalar(
-                    out=turns[:, w * m : w * (m + 1)], in0=turns[:, 0:w], scalar1=10.0 ** (-w * m / 32.0), scalar2=None, op0=ALU.mult
+                    out=turns[:, 2 * w * m : 2 * w * (m + 1)], in0=turns[:, 0 : 2 * w], scalar1=10.0 ** (-w * m / 32.0), scalar2=None, op0=ALU.mult
                 )
-        nc.vector.tensor_scalar(out=turns[:, 64:128], in0=turns[:, 0:64], scalar1=10.0 ** (-2.0), scalar2=None, op0=ALU.mult)
+        nc.vector.tensor_scalar(out=turns[:, 128:256], in0=turns[:, 0:128], scalar1=10.0 ** (-2.0), scalar2=None, op0=ALU.mult)
         halfpi = keep.tile([P, 1], F32, name="halfpi")
-        nc.vector.tensor_scalar(out=halfpi[:], in0=ones[:], scalar1=PI / 2.0, scalar2=None, op0=ALU.mult)
+        nc.vector.tensor_scalar(out=halfpi[:], in0=ones[:, 0:1], scalar1=PI / 2.0, scalar2=None, op0=ALU.mult)
 
         frac = {}
 
         def reduce_angles(name, tb0, tb1):
             n = tb1 - tb0
-            u = keep.tile([P, n, HALF], F32, name="u" + name)
-            k = keep.tile([P, n, HALF], I32, name="k" + name)
-            d = keep.tile([P, n, HALF], F32, name="d" + name)
+            u = keep.tile([P, n, DK], F32, name="u" + name)
+            k = keep.tile([P, n, DK], I32, name="k" + name)
+            d = keep.tile([P, n, DK], F32, name="d" + name)
             for tb in range(tb0, tb1):
                 nc.vector.tensor_scalar(out=u[:, tb - tb0, :], in0=turns[:], scalar1=pos[:, tb : tb + 1], scalar2=None, op0=ALU.mult)
             nc.vector.tensor_copy(out=k[:], in_=u[:])
@@ -157,19 +158,13 @@ def tile_multiheadedattention_pa_kernel(tc, x_words, x_scales, w_words, w_scales
                 frac[tb] = d[:, tb - tb0, :]
 
         reduce_angles("a", 0, 2)
-        reduce_angles("b", 2, 8)
         zero_v(xs47)
-        zero_v(wss[1])
-        zero_v(wss[2])
+        reduce_angles("b", 2, 8)
 
         load_scales(xs47, x_scales, 512, 1024)
         load_codes(xc47a, x_words, 0, 4, 1024, 2048)
         load_codes(xc47b, x_words, 4, 8, 1024, 2048)
-        load_scales(wss[1], w_scales, NW, 2 * NW)
-        load_codes(wcs[1], w_words, 0, G, 2 * NW, 4 * NW)
         nc.sync.dma_start(out=bias1[:], in_=b[NW : NB * NW].partition_broadcast(P))
-        load_scales(wss[2], w_scales, 2 * NW, 3 * NW)
-        load_codes(wcs[2], w_words, 0, G, 4 * NW, 6 * NW)
 
         cos2 = {}
         sin2 = {}
@@ -177,18 +172,10 @@ def tile_multiheadedattention_pa_kernel(tc, x_words, x_scales, w_words, w_scales
         def tables(tb):
             c = keep.tile([P, DK], F32, name="cos%d" % tb)
             s = keep.tile([P, DK], F32, name="sin%d" % tb)
-            mag = work.tile([P, HALF], F32, name="mag")
-            s3 = s[:].rearrange("p (i e) -> p i e", e=2)
+            mag = work.tile([P, DK], F32, name="mag")
             nc.scalar.activation(out=mag[:], in_=frac[tb], func=FUNC.Abs)
-            nc.scalar.activation(out=s3[:, :, 0], in_=frac[tb], func=FUNC.Sin, scale=-2.0 * PI)
-            nc.scalar.activation(out=s3[:, :, 1], in_=frac[tb], func=FUNC.Sin, scale=2.0 * PI)
-            nc.scalar.activation(
-                out=c[:].rearrange("p (i e) -> p i e", e=2),
-                in_=mag[:].unsqueeze(2).to_broadcast([P, HALF, 2]),
-                func=FUNC.Sin,
-                scale=-2.0 * PI,
-                bias=halfpi[:, 0:1],
-            )
+            nc.scalar.activation(out=s[:], in_=frac[tb], func=FUNC.Sin, scale=2.0 * PI)
+            nc.scalar.activation(out=c[:], in_=mag[:], func=FUNC.Sin, scale=-2.0 * PI, bias=halfpi[:, 0:1])
             cos2[tb] = c
             sin2[tb] = s
 
@@ -200,6 +187,7 @@ def tile_multiheadedattention_pa_kernel(tc, x_words, x_scales, w_words, w_scales
         zt = {}
         at = {}
         tt = {}
+        rt = {}
 
         def mx_pass(k, g):
             nb, tb = order[k]
@@ -225,27 +213,38 @@ def tile_multiheadedattention_pa_kernel(tc, x_words, x_scales, w_words, w_scales
             z = zt[k]
             a = work.tile([P, NW], F32, name="a")
             t = work.tile([P, NW], F32, name="t")
+            r = work.tile([P, NW], F32, name="r")
+            nc.vector.tensor_tensor(
+                out=t[:].rearrange("p (h c) -> p h c", h=2),
+                in0=z[:].rearrange("p (h c) -> p h c", h=2),
+                in1=sin2[tb][:].unsqueeze(1).to_broadcast([P, 2, DK]),
+                op=ALU.mult,
+            )
+            nc.scalar.copy(
+                out=r[:, G_COLS:NW].rearrange("p (i e) -> p i e", e=2),
+                in_=t[:, G_COLS:NW].rearrange("p (i e) -> p i e", e=2)[:, :, ::-1],
+            )
             nc.vector.tensor_tensor(
                 out=a[:].rearrange("p (h c) -> p h c", h=2),
                 in0=z[:].rearrange("p (h c) -> p h c", h=2),
                 in1=cos2[tb][:].unsqueeze(1).to_broadcast([P, 2, DK]),
                 op=ALU.mult,
             )
-            nc.vector.tensor_tensor(
-                out=t[:].rearrange("p (h i e) -> p h i e", h=2, e=2),
-                in0=z[:].rearrange("p (h i e) -> p h i e", h=2, e=2)[:, :, :, ::-1],
-                in1=sin2[tb][:].rearrange("p (i e) -> p i e", e=2).unsqueeze(1).to_broadcast([P, 2, HALF, 2]),
-                op=ALU.mult,
-            )
             at[k] = a
             tt[k] = t
+            rt[k] = r
 
         def finish(k):
             nb, tb = order[k]
             o = outp.tile([P, NW], F32, name="o")
-            nc.gpsimd.tensor_tensor(out=o[:, 0:G_COLS], in0=at[k][:, 0:G_COLS], in1=tt[k][:, 0:G_COLS], op=ALU.add)
-            nc.vector.tensor_tensor(out=o[:, G_COLS:NW], in0=at[k][:, G_COLS:NW], in1=tt[k][:, G_COLS:NW], op=ALU.add)
-            nc.scalar.dma_start(
+            nc.gpsimd.tensor_tensor(
+                out=o[:, 0:G_COLS].rearrange("p (i e) -> p i e", e=2),
+                in0=at[k][:, 0:G_COLS].rearrange("p (i e) -> p i e", e=2),
+                in1=tt[k][:, 0:G_COLS].rearrange("p (i e) -> p i e", e=2)[:, :, ::-1],
+                op=ALU.add,
+            )
+            nc.vector.tensor_tensor(out=o[:, G_COLS:NW], in0=at[k][:, G_COLS:NW], in1=rt[k][:, G_COLS:NW], op=ALU.add)
+            nc.sync.dma_start(
                 out=out[0, 2 * nb : 2 * nb + 2, P * tb : P * (tb + 1), :].rearrange("h p j -> p h j"),
                 in_=o[:].rearrange("p (h j) -> p h j", h=2),
             )
@@ -267,8 +266,8 @@ def tile_multiheadedattention_pa_kernel(tc, x_words, x_scales, w_words, w_scales
             add_bias(k)
             if k >= 1:
                 finish(k - 1)
-            if 1 <= k <= NB - 3:
-                nb = k + 2
+            if 1 <= k <= NB - 1:
+                nb = k
                 zero_g(wss[nb])
                 load_scales(wss[nb], w_scales, nb * NW, (nb + 1) * NW)
                 load_codes(wcs[nb], w_words, 0, G, 2 * nb * NW, 2 * (nb + 1) * NW)

@@ -99,9 +99,8 @@ def tile_multiheadedattention_pa_kernel(tc, x_words, x_scales, w_words, w_scales
         def zero_g(plane):
             nc.gpsimd.memset(plane[:].bitcast(F32), 0.0)
 
-        ones = keep.tile([P, 2], F32, name="ones")
-        nc.vector.memset(ones[:, 0:1], 1.0)
-        nc.vector.memset(ones[:, 1:2], -1.0)
+        ones = keep.tile([P, 1], F32, name="ones")
+        nc.vector.memset(ones[:], 1.0)
         zero_v(xs01)
         zero_v(wss[0])
         cold = keep.tile([P, P + NW], BF16, name="cold")
@@ -112,7 +111,7 @@ def tile_multiheadedattention_pa_kernel(tc, x_words, x_scales, w_words, w_scales
         nc.gpsimd.iota(pos[:], pattern=[[P, TB]], base=0, channel_multiplier=1, allow_small_or_imprecise_dtypes=True)
 
         junk = keep.tile([P, 1], F32, name="junk")
-        nc.scalar.activation(out=junk[:], in_=ones[:, 0:1], func=FUNC.Sin)
+        nc.scalar.activation(out=junk[:], in_=ones[:], func=FUNC.Sin)
 
         load_codes(wc0a, w_words, 0, 2, 0, 2 * NW)
         load_codes(xc01a, x_words, 0, 4, 0, 512)
@@ -129,27 +128,27 @@ def tile_multiheadedattention_pa_kernel(tc, x_words, x_scales, w_words, w_scales
             dummy = psum.tile([P, NW], F32, name="acc")
             nc.tensor.matmul(out=dummy[:], lhsT=cold[:, 0:P], rhs=cold[:, P : P + NW], start=True, stop=True)
 
-        turns = keep.tile([P, DK], F32, name="turns")
+        turns = keep.tile([P, HALF], F32, name="turns")
         for j in range(4):
             nc.vector.tensor_scalar(
-                out=turns[:, 2 * j : 2 * j + 2], in0=ones[:], scalar1=10.0 ** (-j / 32.0) / (2.0 * PI), scalar2=None, op0=ALU.mult
+                out=turns[:, j : j + 1], in0=ones[:], scalar1=10.0 ** (-j / 32.0) / (2.0 * PI), scalar2=None, op0=ALU.mult
             )
         for w in (4, 16):
             for m in range(1, 4):
                 nc.vector.tensor_scalar(
-                    out=turns[:, 2 * w * m : 2 * w * (m + 1)], in0=turns[:, 0 : 2 * w], scalar1=10.0 ** (-w * m / 32.0), scalar2=None, op0=ALU.mult
+                    out=turns[:, w * m : w * (m + 1)], in0=turns[:, 0:w], scalar1=10.0 ** (-w * m / 32.0), scalar2=None, op0=ALU.mult
                 )
-        nc.vector.tensor_scalar(out=turns[:, 128:256], in0=turns[:, 0:128], scalar1=10.0 ** (-2.0), scalar2=None, op0=ALU.mult)
+        nc.vector.tensor_scalar(out=turns[:, 64:128], in0=turns[:, 0:64], scalar1=10.0 ** (-2.0), scalar2=None, op0=ALU.mult)
         halfpi = keep.tile([P, 1], F32, name="halfpi")
-        nc.vector.tensor_scalar(out=halfpi[:], in0=ones[:, 0:1], scalar1=PI / 2.0, scalar2=None, op0=ALU.mult)
+        nc.vector.tensor_scalar(out=halfpi[:], in0=ones[:], scalar1=PI / 2.0, scalar2=None, op0=ALU.mult)
 
         frac = {}
 
         def reduce_angles(name, tb0, tb1):
             n = tb1 - tb0
-            u = keep.tile([P, n, DK], F32, name="u" + name)
-            k = keep.tile([P, n, DK], I32, name="k" + name)
-            d = keep.tile([P, n, DK], F32, name="d" + name)
+            u = keep.tile([P, n, HALF], F32, name="u" + name)
+            k = keep.tile([P, n, HALF], I32, name="k" + name)
+            d = keep.tile([P, n, HALF], F32, name="d" + name)
             for tb in range(tb0, tb1):
                 nc.vector.tensor_scalar(out=u[:, tb - tb0, :], in0=turns[:], scalar1=pos[:, tb : tb + 1], scalar2=None, op0=ALU.mult)
             nc.vector.tensor_copy(out=k[:], in_=u[:])
@@ -160,11 +159,17 @@ def tile_multiheadedattention_pa_kernel(tc, x_words, x_scales, w_words, w_scales
         reduce_angles("a", 0, 2)
         zero_v(xs47)
         reduce_angles("b", 2, 8)
+        zero_v(wss[1])
+        zero_v(wss[2])
 
         load_scales(xs47, x_scales, 512, 1024)
         load_codes(xc47a, x_words, 0, 4, 1024, 2048)
         load_codes(xc47b, x_words, 4, 8, 1024, 2048)
+        load_scales(wss[1], w_scales, NW, 2 * NW)
+        load_codes(wcs[1], w_words, 0, G, 2 * NW, 4 * NW)
         nc.sync.dma_start(out=bias1[:], in_=b[NW : NB * NW].partition_broadcast(P))
+        load_scales(wss[2], w_scales, 2 * NW, 3 * NW)
+        load_codes(wcs[2], w_words, 0, G, 4 * NW, 6 * NW)
 
         cos2 = {}
         sin2 = {}
@@ -172,10 +177,18 @@ def tile_multiheadedattention_pa_kernel(tc, x_words, x_scales, w_words, w_scales
         def tables(tb):
             c = keep.tile([P, DK], F32, name="cos%d" % tb)
             s = keep.tile([P, DK], F32, name="sin%d" % tb)
-            mag = work.tile([P, DK], F32, name="mag")
+            mag = work.tile([P, HALF], F32, name="mag")
+            s3 = s[:].rearrange("p (i e) -> p i e", e=2)
             nc.scalar.activation(out=mag[:], in_=frac[tb], func=FUNC.Abs)
-            nc.scalar.activation(out=s[:], in_=frac[tb], func=FUNC.Sin, scale=2.0 * PI)
-            nc.scalar.activation(out=c[:], in_=mag[:], func=FUNC.Sin, scale=-2.0 * PI, bias=halfpi[:, 0:1])
+            nc.scalar.activation(out=s3[:, :, 0], in_=frac[tb], func=FUNC.Sin, scale=2.0 * PI)
+            nc.scalar.activation(out=s3[:, :, 1], in_=frac[tb], func=FUNC.Sin, scale=-2.0 * PI)
+            nc.scalar.activation(
+                out=c[:].rearrange("p (i e) -> p i e", e=2),
+                in_=mag[:].unsqueeze(2).to_broadcast([P, HALF, 2]),
+                func=FUNC.Sin,
+                scale=-2.0 * PI,
+                bias=halfpi[:, 0:1],
+            )
             cos2[tb] = c
             sin2[tb] = s
 
@@ -186,7 +199,6 @@ def tile_multiheadedattention_pa_kernel(tc, x_words, x_scales, w_words, w_scales
         acc = {}
         zt = {}
         at = {}
-        tt = {}
         rt = {}
 
         def mx_pass(k, g):
@@ -208,68 +220,74 @@ def tile_multiheadedattention_pa_kernel(tc, x_words, x_scales, w_words, w_scales
             nc.vector.tensor_tensor(out=z[:], in0=acc[k][:], in1=bias, op=ALU.add)
             zt[k] = z
 
-        def products(k):
+        def sine_product(k):
             nb, tb = order[k]
-            z = zt[k]
-            a = work.tile([P, NW], F32, name="a")
             t = work.tile([P, NW], F32, name="t")
             r = work.tile([P, NW], F32, name="r")
             nc.vector.tensor_tensor(
                 out=t[:].rearrange("p (h c) -> p h c", h=2),
-                in0=z[:].rearrange("p (h c) -> p h c", h=2),
+                in0=zt[k][:].rearrange("p (h c) -> p h c", h=2),
                 in1=sin2[tb][:].unsqueeze(1).to_broadcast([P, 2, DK]),
                 op=ALU.mult,
             )
             nc.scalar.copy(
-                out=r[:, G_COLS:NW].rearrange("p (i e) -> p i e", e=2),
-                in_=t[:, G_COLS:NW].rearrange("p (i e) -> p i e", e=2)[:, :, ::-1],
+                out=r[:].rearrange("p (i e) -> p i e", e=2),
+                in_=t[:].rearrange("p (i e) -> p i e", e=2)[:, :, ::-1],
             )
+            rt[k] = r
+
+        def cosine_product(k):
+            nb, tb = order[k]
+            a = work.tile([P, NW], F32, name="a")
             nc.vector.tensor_tensor(
                 out=a[:].rearrange("p (h c) -> p h c", h=2),
-                in0=z[:].rearrange("p (h c) -> p h c", h=2),
+                in0=zt[k][:].rearrange("p (h c) -> p h c", h=2),
                 in1=cos2[tb][:].unsqueeze(1).to_broadcast([P, 2, DK]),
                 op=ALU.mult,
             )
             at[k] = a
-            tt[k] = t
-            rt[k] = r
 
-        def finish(k):
+        def finish(k, g_cols):
             nb, tb = order[k]
             o = outp.tile([P, NW], F32, name="o")
-            nc.gpsimd.tensor_tensor(
-                out=o[:, 0:G_COLS].rearrange("p (i e) -> p i e", e=2),
-                in0=at[k][:, 0:G_COLS].rearrange("p (i e) -> p i e", e=2),
-                in1=tt[k][:, 0:G_COLS].rearrange("p (i e) -> p i e", e=2)[:, :, ::-1],
-                op=ALU.add,
-            )
-            nc.vector.tensor_tensor(out=o[:, G_COLS:NW], in0=at[k][:, G_COLS:NW], in1=rt[k][:, G_COLS:NW], op=ALU.add)
-            nc.sync.dma_start(
+            if g_cols > 0:
+                nc.gpsimd.tensor_tensor(out=o[:, 0:g_cols], in0=at[k][:, 0:g_cols], in1=rt[k][:, 0:g_cols], op=ALU.add)
+            nc.vector.tensor_tensor(out=o[:, g_cols:NW], in0=at[k][:, g_cols:NW], in1=rt[k][:, g_cols:NW], op=ALU.add)
+            nc.scalar.dma_start(
                 out=out[0, 2 * nb : 2 * nb + 2, P * tb : P * (tb + 1), :].rearrange("h p j -> p h j"),
                 in_=o[:].rearrange("p (h j) -> p h j", h=2),
             )
 
-        for k in range(len(order)):
-            if k == 0:
+        n_tiles = len(order)
+        for j in range(n_tiles + 2):
+            if j == 0:
                 acc[0] = psum.tile([P, NW], F32, name="acc")
                 acc[1] = psum.tile([P, NW], F32, name="acc")
                 for gs in ((0, 1), (2, 3), (4,), (5, 6, 7)):
                     for kk in (0, 1):
                         for g in gs:
                             mx_pass(kk, g)
-            elif k > 1:
-                acc[k] = psum.tile([P, NW], F32, name="acc")
+            elif 1 < j < n_tiles:
+                acc[j] = psum.tile([P, NW], F32, name="acc")
                 for g in range(G):
-                    mx_pass(k, g)
-            if k + 3 < TB:
-                tables(k + 3)
-            add_bias(k)
-            if k >= 1:
-                finish(k - 1)
-            if 1 <= k <= NB - 1:
-                nb = k
+                    mx_pass(j, g)
+            if j + 3 < TB:
+                tables(j + 3)
+            if j < n_tiles:
+                add_bias(j)
+            if j == n_tiles:
+                cosine_product(j - 1)
+            if j >= 2:
+                finish(j - 2, G_COLS if j < n_tiles else 0)
+            if 2 <= j <= NB - 2:
+                nb = j + 1
                 zero_g(wss[nb])
                 load_scales(wss[nb], w_scales, nb * NW, (nb + 1) * NW)
                 load_codes(wcs[nb], w_words, 0, G, 2 * nb * NW, 2 * (nb + 1) * NW)
-            products(k)
-        finish(len(order) - 1)
+            if j == n_tiles - 1:
+                sine_product(j)
+                cosine_product(j - 1)
+            elif j < n_tiles - 1:
+                if j >= 1:
+                    cosine_product(j - 1)
+                sine_product(j)

@@ -20,7 +20,7 @@ HALF = DK // 2
 FLOPS = 2 * 1024 * 4096 * 4096
 
 PI = 3.141592653589793
-G_COLS = 128
+G_COLS = 192
 WARM = 6
 
 
@@ -252,6 +252,12 @@ def tile_multiheadedattention_pa_kernel(tc, x_words, x_scales, w_words, w_scales
             o = outp.tile([P, NW], F32, name="o")
             if g_cols > 0:
                 nc.gpsimd.tensor_tensor(out=o[:, 0:g_cols], in0=at[k][:, 0:g_cols], in1=rt[k][:, 0:g_cols], op=ALU.add)
+            if k == n_tiles - 1:
+                for h in range(2):
+                    cols = slice(h * DK, (h + 1) * DK)
+                    nc.vector.tensor_tensor(out=o[:, cols], in0=at[k][:, cols], in1=rt[k][:, cols], op=ALU.add)
+                    nc.scalar.dma_start(out=out[0, 2 * nb + h, P * tb : P * (tb + 1), :], in_=o[:, cols])
+                return
             nc.vector.tensor_tensor(out=o[:, g_cols:NW], in0=at[k][:, g_cols:NW], in1=rt[k][:, g_cols:NW], op=ALU.add)
             nc.scalar.dma_start(
                 out=out[0, 2 * nb : 2 * nb + 2, P * tb : P * (tb + 1), :].rearrange("h p j -> p h j"),

@@ -39,27 +39,27 @@ def tile_multiheadedattention_pa_kernel(tc, x_words, x_scales, w_words, w_scales
         w_scale = {}
 
         def x_code_tile(name, g0, g1, tb0, tb1):
-            t = keep.tile([P, g1 - g0, 256 * (tb1 - tb0)], U8, name=name, align_bytes=64)
+            t = keep.tile([P, g1 - g0, 256 * (tb1 - tb0)], U8, name=name, align_bytes=256)
             for g in range(g0, g1):
                 for tb in range(tb0, tb1):
                     x_codes[(tb, g)] = t[:, g - g0, 256 * (tb - tb0) : 256 * (tb - tb0 + 1)]
             return t
 
         def x_plane_tile(name, tb0, tb1):
-            t = keep.tile([P, G, P * (tb1 - tb0)], U8, name=name, align_bytes=64)
+            t = keep.tile([P, G, P * (tb1 - tb0)], U8, name=name, align_bytes=256)
             for g in range(G):
                 for tb in range(tb0, tb1):
                     x_scale[(tb, g)] = t[:, g, P * (tb - tb0) : P * (tb - tb0 + 1)]
             return t
 
         def w_code_tile(name, nb, g0, g1):
-            t = keep.tile([P, g1 - g0, 2 * NW], U8, name=name, align_bytes=64)
+            t = keep.tile([P, g1 - g0, 2 * NW], U8, name=name, align_bytes=256)
             for g in range(g0, g1):
                 w_codes[(nb, g)] = t[:, g - g0, :]
             return t
 
         def w_plane_tile(name, nb):
-            t = keep.tile([P, G, NW], U8, name=name, align_bytes=64)
+            t = keep.tile([P, G, NW], U8, name=name, align_bytes=256)
             for g in range(G):
                 w_scale[(nb, g)] = t[:, g, :]
             return t

@@ -1,6 +1,7 @@
 from contextlib import ExitStack
 
 import concourse.mybir as mybir
+from concourse.masks import make_identity
 
 F32 = mybir.dt.float32
 BF16 = mybir.dt.bfloat16
@@ -22,6 +23,7 @@ FLOPS = 2 * 1024 * 4096 * 4096
 PI = 3.141592653589793
 G_COLS = 192
 WARM = 6
+HALVES = 1
 
 
 def tile_multiheadedattention_pa_kernel(tc, x_words, x_scales, w_words, w_scales, b, out):
@@ -30,7 +32,8 @@ def tile_multiheadedattention_pa_kernel(tc, x_words, x_scales, w_words, w_scales
         keep = ctx.enter_context(tc.tile_pool(name="keep", bufs=1))
         work = ctx.enter_context(tc.tile_pool(name="work", bufs=3))
         outp = ctx.enter_context(tc.tile_pool(name="outp", bufs=6))
-        psum = ctx.enter_context(tc.psum_pool(name="psum", bufs=8))
+        psum = ctx.enter_context(tc.psum_pool(name="psum", bufs=7))
+        tabs = ctx.enter_context(tc.psum_pool(name="tabs", bufs=1))
         ctx.enter_context(tc.manual_schedule())
 
         x_codes = {}
@@ -105,10 +108,11 @@ def tile_multiheadedattention_pa_kernel(tc, x_words, x_scales, w_words, w_scales
         zero_v(wss[0])
         cold = keep.tile([P, P + NW], BF16, name="cold")
         nc.vector.memset(cold[:], 0.0)
-        zero_v(xs23)
 
         pos = keep.tile([P, TB], F32, name="pos")
         nc.gpsimd.iota(pos[:], pattern=[[P, TB]], base=0, channel_multiplier=1, allow_small_or_imprecise_dtypes=True)
+        ident = keep.tile([P, P], F32, name="ident")
+        make_identity(nc, ident[:])
 
         junk = keep.tile([P, 1], F32, name="junk")
         nc.scalar.activation(out=junk[:], in_=ones[:], func=FUNC.Sin)
@@ -121,8 +125,6 @@ def tile_multiheadedattention_pa_kernel(tc, x_words, x_scales, w_words, w_scales
         load_codes(xc01b, x_words, 4, 8, 0, 512)
         load_codes(wc0c, w_words, 5, 8, 0, 2 * NW)
         nc.sync.dma_start(out=bias0[:], in_=b[0:NW].partition_broadcast(P))
-        load_scales(xs23, x_scales, 256, 512)
-        load_codes(xc23, x_words, 0, 8, 512, 1024)
 
         for i in range(WARM):
             dummy = psum.tile([P, NW], F32, name="acc")
@@ -143,22 +145,58 @@ def tile_multiheadedattention_pa_kernel(tc, x_words, x_scales, w_words, w_scales
         nc.vector.tensor_scalar(out=halfpi[:], in0=ones[:], scalar1=PI / 2.0, scalar2=None, op0=ALU.mult)
 
         frac = {}
+        size = {}
 
         def reduce_angles(name, tb0, tb1):
             n = tb1 - tb0
             u = keep.tile([P, n, HALF], F32, name="u" + name)
             k = keep.tile([P, n, HALF], I32, name="k" + name)
             d = keep.tile([P, n, HALF], F32, name="d" + name)
+            a = keep.tile([P, n, HALF], F32, name="m" + name)
             for tb in range(tb0, tb1):
                 nc.vector.tensor_scalar(out=u[:, tb - tb0, :], in0=turns[:], scalar1=pos[:, tb : tb + 1], scalar2=None, op0=ALU.mult)
             nc.vector.tensor_copy(out=k[:], in_=u[:])
             nc.vector.tensor_tensor(out=d[:], in0=u[:], in1=k[:], op=ALU.subtract)
+            nc.vector.scalar_tensor_tensor(out=a[:], in0=d[:], scalar=-1.0, in1=d[:], op0=ALU.mult, op1=ALU.max)
             for tb in range(tb0, tb1):
                 frac[tb] = d[:, tb - tb0, :]
+                size[tb] = a[:, tb - tb0, :]
 
+        cos2 = {}
+        sin2 = {}
+        both = {}
+
+        def tables(tb):
+            cs = keep.tile([P, 2 * DK], F32, name="cs%d" % tb)
+            c = cs[:, 0:DK]
+            s = cs[:, DK : 2 * DK]
+            s3 = s.rearrange("p (i e) -> p i e", e=2)
+            nc.scalar.activation(out=s3[:, :, 0], in_=frac[tb], func=FUNC.Sin, scale=2.0 * PI)
+            nc.scalar.activation(out=s3[:, :, 1], in_=frac[tb], func=FUNC.Sin, scale=-2.0 * PI)
+            nc.scalar.activation(
+                out=c.rearrange("p (i e) -> p i e", e=2),
+                in_=size[tb].unsqueeze(2).to_broadcast([P, HALF, 2]),
+                func=FUNC.Sin,
+                scale=-2.0 * PI,
+                bias=halfpi[:, 0:1],
+            )
+            cos2[tb] = c
+            sin2[tb] = s
+            both[tb] = cs
+
+        LAST = TB - 1
+        reduce_angles("c", LAST, TB)
+        tables(LAST)
+        tabp = tabs.tile([P, 2 * DK], F32, name="tabp")
+        nc.tensor.matmul(out=tabp[:, DK : 2 * DK], lhsT=ident[:], rhs=sin2[LAST], start=True, stop=True)
+        nc.tensor.matmul(out=tabp[:, 0:DK], lhsT=ident[:], rhs=cos2[LAST], start=True, stop=True)
+
+        zero_v(xs23)
+        load_scales(xs23, x_scales, 256, 512)
+        load_codes(xc23, x_words, 0, 8, 512, 1024)
         reduce_angles("a", 0, 2)
         zero_v(xs47)
-        reduce_angles("b", 2, 8)
+        reduce_angles("b", 2, LAST)
         zero_v(wss[1])
         zero_v(wss[2])
 
@@ -171,129 +209,138 @@ def tile_multiheadedattention_pa_kernel(tc, x_words, x_scales, w_words, w_scales
         load_scales(wss[2], w_scales, 2 * NW, 3 * NW)
         load_codes(wcs[2], w_words, 0, G, 4 * NW, 6 * NW)
 
-        cos2 = {}
-        sin2 = {}
-
-        def tables(tb):
-            c = keep.tile([P, DK], F32, name="cos%d" % tb)
-            s = keep.tile([P, DK], F32, name="sin%d" % tb)
-            mag = work.tile([P, HALF], F32, name="mag")
-            s3 = s[:].rearrange("p (i e) -> p i e", e=2)
-            nc.scalar.activation(out=mag[:], in_=frac[tb], func=FUNC.Abs)
-            nc.scalar.activation(out=s3[:, :, 0], in_=frac[tb], func=FUNC.Sin, scale=2.0 * PI)
-            nc.scalar.activation(out=s3[:, :, 1], in_=frac[tb], func=FUNC.Sin, scale=-2.0 * PI)
-            nc.scalar.activation(
-                out=c[:].rearrange("p (i e) -> p i e", e=2),
-                in_=mag[:].unsqueeze(2).to_broadcast([P, HALF, 2]),
-                func=FUNC.Sin,
-                scale=-2.0 * PI,
-                bias=halfpi[:, 0:1],
-            )
-            cos2[tb] = c
-            sin2[tb] = s
-
         for tb in range(3):
             tables(tb)
 
-        order = [(nb, tb) for nb in range(NB) for tb in range(TB)]
-        acc = {}
+        order = [(nb, tb) for nb in range(NB) for tb in range(LAST)]
+        n_main = len(order)
         zt = {}
+        tt = {}
         at = {}
         rt = {}
+        ot = {}
 
-        def mx_pass(k, g):
-            nb, tb = order[k]
+        def mx_pass(nb, tb, g, sums, c0, c1):
             nc.tensor.matmul_mx(
-                out=acc[k][:],
+                out=sums[:],
                 lhsT=x_codes[(tb, g)].bitcast(FP4X4),
                 lhsT_scale=x_scale[(tb, g)],
-                rhs=w_codes[(nb, g)].bitcast(FP4X4),
-                rhs_scale=w_scale[(nb, g)],
+                rhs=w_codes[(nb, g)][:, 2 * c0 : 2 * c1].bitcast(FP4X4),
+                rhs_scale=w_scale[(nb, g)][:, c0:c1],
                 start=(g == 0),
                 stop=(g == G - 1),
             )
 
+        def by_head(ap):
+            return ap.rearrange("p (h c) -> p h c", c=DK)
+
+        def by_pair(ap):
+            return ap.rearrange("p (i e) -> p i e", e=2)
+
+        def bias_of(nb, c0, c1):
+            return bias0[:, c0:c1] if nb == 0 else bias1[:, (nb - 1) * NW + c0 : (nb - 1) * NW + c1]
+
         def add_bias(k):
-            nb, tb = order[k]
-            z = work.tile([P, NW], F32, name="z")
-            bias = bias0[:] if nb == 0 else bias1[:, (nb - 1) * NW : nb * NW]
-            nc.vector.tensor_tensor(out=z[:], in0=acc[k][:], in1=bias, op=ALU.add)
-            zt[k] = z
+            zt[k] = work.tile([P, NW], F32, name="z")
+            nc.vector.tensor_tensor(out=zt[k][:], in0=acc[k][:], in1=bias_of(order[k][0], 0, NW), op=ALU.add)
+
+        def product(dst, k, table):
+            nc.vector.tensor_tensor(
+                out=by_head(dst[:]), in0=by_head(zt[k][:]), in1=table.unsqueeze(1).to_broadcast([P, 2, DK]), op=ALU.mult
+            )
 
         def sine_product(k):
-            nb, tb = order[k]
-            t = work.tile([P, NW], F32, name="t")
-            r = work.tile([P, NW], F32, name="r")
-            nc.vector.tensor_tensor(
-                out=t[:].rearrange("p (h c) -> p h c", h=2),
-                in0=zt[k][:].rearrange("p (h c) -> p h c", h=2),
-                in1=sin2[tb][:].unsqueeze(1).to_broadcast([P, 2, DK]),
-                op=ALU.mult,
-            )
-            nc.scalar.copy(
-                out=r[:].rearrange("p (i e) -> p i e", e=2),
-                in_=t[:].rearrange("p (i e) -> p i e", e=2)[:, :, ::-1],
-            )
-            rt[k] = r
+            tt[k] = work.tile([P, NW], F32, name="t")
+            rt[k] = work.tile([P, NW], F32, name="r")
+            product(tt[k], k, sin2[order[k][1]])
+            nc.scalar.copy(out=by_pair(rt[k][:]), in_=by_pair(tt[k][:])[:, :, ::-1])
 
         def cosine_product(k):
-            nb, tb = order[k]
-            a = work.tile([P, NW], F32, name="a")
-            nc.vector.tensor_tensor(
-                out=a[:].rearrange("p (h c) -> p h c", h=2),
-                in0=zt[k][:].rearrange("p (h c) -> p h c", h=2),
-                in1=cos2[tb][:].unsqueeze(1).to_broadcast([P, 2, DK]),
-                op=ALU.mult,
-            )
-            at[k] = a
+            at[k] = work.tile([P, NW], F32, name="a")
+            product(at[k], k, cos2[order[k][1]])
 
-        def finish(k, g_cols):
-            nb, tb = order[k]
+        def store(queue, o, nb, tb, c0, c1):
+            queue.dma_start(
+                out=out[0, 2 * nb + c0 // DK : 2 * nb + c1 // DK, P * tb : P * (tb + 1), :].rearrange("h p j -> p h j"),
+                in_=by_head(o[:]),
+            )
+
+        def finish(k, g_cols, queue):
             o = outp.tile([P, NW], F32, name="o")
-            if g_cols > 0:
-                nc.gpsimd.tensor_tensor(out=o[:, 0:g_cols], in0=at[k][:, 0:g_cols], in1=rt[k][:, 0:g_cols], op=ALU.add)
-            if k == n_tiles - 1:
-                for h in range(2):
-                    cols = slice(h * DK, (h + 1) * DK)
-                    nc.vector.tensor_tensor(out=o[:, cols], in0=at[k][:, cols], in1=rt[k][:, cols], op=ALU.add)
-                    nc.scalar.dma_start(out=out[0, 2 * nb + h, P * tb : P * (tb + 1), :], in_=o[:, cols])
-                return
-            nc.vector.tensor_tensor(out=o[:, g_cols:NW], in0=at[k][:, g_cols:NW], in1=rt[k][:, g_cols:NW], op=ALU.add)
-            nc.scalar.dma_start(
-                out=out[0, 2 * nb : 2 * nb + 2, P * tb : P * (tb + 1), :].rearrange("h p j -> p h j"),
-                in_=o[:].rearrange("p (h j) -> p h j", h=2),
-            )
+            nc.gpsimd.tensor_tensor(out=o[:, 0:g_cols], in0=at[k][:, 0:g_cols], in1=rt[k][:, 0:g_cols], op=ALU.add)
+            if g_cols < NW:
+                nc.vector.tensor_tensor(out=o[:, g_cols:NW], in0=at[k][:, g_cols:NW], in1=rt[k][:, g_cols:NW], op=ALU.add)
+            store(queue, o, order[k][0], order[k][1], 0, NW)
 
-        n_tiles = len(order)
-        for j in range(n_tiles + 2):
+        acc = {}
+        for j in range(n_main):
+            nb, tb = order[j]
             if j == 0:
                 acc[0] = psum.tile([P, NW], F32, name="acc")
                 acc[1] = psum.tile([P, NW], F32, name="acc")
                 for gs in ((0, 1), (2, 3), (4,), (5, 6, 7)):
                     for kk in (0, 1):
                         for g in gs:
-                            mx_pass(kk, g)
-            elif 1 < j < n_tiles:
+                            mx_pass(0, kk, g, acc[kk], 0, NW)
+            elif j > 1:
                 acc[j] = psum.tile([P, NW], F32, name="acc")
                 for g in range(G):
-                    mx_pass(j, g)
-            if j + 3 < TB:
+                    mx_pass(nb, tb, g, acc[j], 0, NW)
+            if j + 3 < LAST:
                 tables(j + 3)
-            if j < n_tiles:
-                add_bias(j)
-            if j == n_tiles:
-                cosine_product(j - 1)
+            add_bias(j)
             if j >= 2:
-                finish(j - 2, G_COLS if j < n_tiles else 0)
+                finish(j - 2, G_COLS, nc.scalar)
             if 2 <= j <= NB - 2:
-                nb = j + 1
-                zero_g(wss[nb])
-                load_scales(wss[nb], w_scales, nb * NW, (nb + 1) * NW)
-                load_codes(wcs[nb], w_words, 0, G, 2 * nb * NW, 2 * (nb + 1) * NW)
-            if j == n_tiles - 1:
-                sine_product(j)
+                nxt = j + 1
+                zero_g(wss[nxt])
+                load_scales(wss[nxt], w_scales, nxt * NW, (nxt + 1) * NW)
+                load_codes(wcs[nxt], w_words, 0, G, 2 * nxt * NW, 2 * (nxt + 1) * NW)
+            if j >= 1:
                 cosine_product(j - 1)
-            elif j < n_tiles - 1:
-                if j >= 1:
-                    cosine_product(j - 1)
-                sine_product(j)
+            sine_product(j)
+
+        units = [(nb, 0, NW) for nb in range(NB - HALVES)]
+        for nb in range(NB - HALVES, NB):
+            units.extend([(nb, 0, DK), (nb, DK, NW)])
+        n_units = len(units)
+        for i in range(n_units):
+            nb, c0, c1 = units[i]
+            wide = c1 - c0
+            nh = wide // DK
+            sums = psum.tile([P, wide], F32, name="acc")
+            for g in range(G):
+                mx_pass(nb, LAST, g, sums, c0, c1)
+            z = work.tile([P, wide], F32, name="z")
+            nc.vector.tensor_tensor(out=z[:], in0=sums[:], in1=bias_of(nb, c0, c1), op=ALU.add)
+            if i == 0:
+                finish(n_main - 2, G_COLS, nc.scalar)
+                cosine_product(n_main - 1)
+            sc = work.tile([P, 2, wide], F32, name="sc")
+            r = work.tile([P, wide], F32, name="r")
+            o = outp.tile([P, wide], F32, name="o")
+            if i < n_units - 1:
+                nc.vector.tensor_tensor(
+                    out=sc[:].rearrange("p t (h c) -> p t h c", h=nh),
+                    in0=by_head(z[:]).unsqueeze(1).to_broadcast([P, 2, nh, DK]),
+                    in1=tabp[:].rearrange("p (t c) -> p t c", t=2).unsqueeze(2).to_broadcast([P, 2, nh, DK]),
+                    op=ALU.mult,
+                )
+                nc.scalar.copy(out=by_pair(r[:]), in_=by_pair(sc[:, 1, :])[:, :, ::-1])
+            else:
+                nc.vector.tensor_tensor(out=sc[:, 0, :], in0=z[:], in1=tabp[:, 0:DK], op=ALU.mult)
+                nc.vector.tensor_tensor(
+                    out=by_pair(r[:]), in0=by_pair(z[:])[:, :, ::-1], in1=by_pair(tabp[:, DK : 2 * DK])[:, :, ::-1], op=ALU.mult
+                )
+                nc.vector.tensor_tensor(out=held[2][:], in0=held[0][:, 0, :], in1=held[1][:], op=ALU.add)
+                store(nc.sync, held[2], nb, LAST, 0, DK)
+            if i == 0:
+                finish(n_main - 1, NW, nc.sync)
+            if i < n_units - 2:
+                nc.gpsimd.tensor_tensor(out=o[:], in0=sc[:, 0, :], in1=r[:], op=ALU.add)
+                store(nc.sync, o, nb, LAST, c0, c1)
+            elif i == n_units - 2:
+                held = (sc, r, o)
+            else:
+                nc.vector.tensor_tensor(out=o[:], in0=sc[:, 0, :], in1=r[:], op=ALU.add)
+                store(nc.scalar, o, nb, LAST, c0, c1)

@@ -23,7 +23,6 @@ FLOPS = 2 * 1024 * 4096 * 4096
 PI = 3.141592653589793
 G_COLS = 192
 WARM = 6
-HALVES = 1
 
 
 def tile_multiheadedattention_pa_kernel(tc, x_words, x_scales, w_words, w_scales, b, out):
@@ -300,47 +299,56 @@ def tile_multiheadedattention_pa_kernel(tc, x_words, x_scales, w_words, w_scales
                 cosine_product(j - 1)
             sine_product(j)
 
-        units = [(nb, 0, NW) for nb in range(NB - HALVES)]
-        for nb in range(NB - HALVES, NB):
-            units.extend([(nb, 0, DK), (nb, DK, NW)])
-        n_units = len(units)
-        for i in range(n_units):
-            nb, c0, c1 = units[i]
-            wide = c1 - c0
-            nh = wide // DK
-            sums = psum.tile([P, wide], F32, name="acc")
+        def sums_of(nb, c0, c1):
+            sums = psum.tile([P, c1 - c0], F32, name="acc")
             for g in range(G):
                 mx_pass(nb, LAST, g, sums, c0, c1)
-            z = work.tile([P, wide], F32, name="z")
+            return sums
+
+        def biased(nb, c0, c1, sums):
+            z = work.tile([P, c1 - c0], F32, name="z")
             nc.vector.tensor_tensor(out=z[:], in0=sums[:], in1=bias_of(nb, c0, c1), op=ALU.add)
-            if i == 0:
-                finish(n_main - 2, G_COLS, nc.scalar)
-                cosine_product(n_main - 1)
+            return z
+
+        def both_products(z, wide):
+            nh = wide // DK
             sc = work.tile([P, 2, wide], F32, name="sc")
             r = work.tile([P, wide], F32, name="r")
-            o = outp.tile([P, wide], F32, name="o")
-            if i < n_units - 1:
-                nc.vector.tensor_tensor(
-                    out=sc[:].rearrange("p t (h c) -> p t h c", h=nh),
-                    in0=by_head(z[:]).unsqueeze(1).to_broadcast([P, 2, nh, DK]),
-                    in1=tabp[:].rearrange("p (t c) -> p t c", t=2).unsqueeze(2).to_broadcast([P, 2, nh, DK]),
-                    op=ALU.mult,
-                )
-                nc.scalar.copy(out=by_pair(r[:]), in_=by_pair(sc[:, 1, :])[:, :, ::-1])
-            else:
-                nc.vector.tensor_tensor(out=sc[:, 0, :], in0=z[:], in1=tabp[:, 0:DK], op=ALU.mult)
-                nc.vector.tensor_tensor(
-                    out=by_pair(r[:]), in0=by_pair(z[:])[:, :, ::-1], in1=by_pair(tabp[:, DK : 2 * DK])[:, :, ::-1], op=ALU.mult
-                )
-                nc.vector.tensor_tensor(out=held[2][:], in0=held[0][:, 0, :], in1=held[1][:], op=ALU.add)
-                store(nc.sync, held[2], nb, LAST, 0, DK)
-            if i == 0:
+            nc.vector.tensor_tensor(
+                out=sc[:].rearrange("p t (h c) -> p t h c", h=nh),
+                in0=by_head(z[:]).unsqueeze(1).to_broadcast([P, 2, nh, DK]),
+                in1=tabp[:].rearrange("p (t c) -> p t c", t=2).unsqueeze(2).to_broadcast([P, 2, nh, DK]),
+                op=ALU.mult,
+            )
+            nc.scalar.copy(out=by_pair(r[:]), in_=by_pair(sc[:, 1, :])[:, :, ::-1])
+            return sc, r
+
+        def add_and_store(engine, queue, a, r, nb, c0, c1):
+            o = outp.tile([P, c1 - c0], F32, name="o")
+            engine.tensor_tensor(out=o[:], in0=a, in1=r[:], op=ALU.add)
+            store(queue, o, nb, LAST, c0, c1)
+
+        for nb in range(NB - 1):
+            z = biased(nb, 0, NW, sums_of(nb, 0, NW))
+            if nb == 0:
+                finish(n_main - 2, G_COLS, nc.scalar)
+                cosine_product(n_main - 1)
+            sc, r = both_products(z, NW)
+            if nb == 0:
                 finish(n_main - 1, NW, nc.sync)
-            if i < n_units - 2:
-                nc.gpsimd.tensor_tensor(out=o[:], in0=sc[:, 0, :], in1=r[:], op=ALU.add)
-                store(nc.sync, o, nb, LAST, c0, c1)
-            elif i == n_units - 2:
-                held = (sc, r, o)
-            else:
-                nc.vector.tensor_tensor(out=o[:], in0=sc[:, 0, :], in1=r[:], op=ALU.add)
-                store(nc.scalar, o, nb, LAST, c0, c1)
+            add_and_store(nc.gpsimd, nc.sync, sc[:, 0, :], r, nb, 0, NW)
+
+        nb = NB - 1
+        sums0 = sums_of(nb, 0, DK)
+        sums1 = sums_of(nb, DK, NW)
+        z0 = biased(nb, 0, DK, sums0)
+        z1 = biased(nb, DK, NW, sums1)
+        sc0, r0 = both_products(z0, DK)
+        a1 = work.tile([P, DK], F32, name="a")
+        r1 = work.tile([P, DK], F32, name="r")
+        nc.vector.tensor_tensor(out=a1[:], in0=z1[:], in1=tabp[:, 0:DK], op=ALU.mult)
+        nc.vector.tensor_tensor(
+            out=by_pair(r1[:]), in0=by_pair(z1[:])[:, :, ::-1], in1=by_pair(tabp[:, DK : 2 * DK])[:, :, ::-1], op=ALU.mult
+        )
+        add_and_store(nc.vector, nc.sync, sc0[:, 0, :], r0, nb, 0, DK)
+        add_and_store(nc.vector, nc.scalar, a1[:], r1, nb, DK, NW)

@@ -187,8 +187,6 @@ def tile_multiheadedattention_pa_kernel(tc, x_words, x_scales, w_words, w_scales
         reduce_angles("c", LAST, TB)
         tables(LAST)
         tabp = tabs.tile([P, 2 * DK], F32, name="tabp")
-        nc.tensor.matmul(out=tabp[:, DK : 2 * DK], lhsT=ident[:], rhs=sin2[LAST], start=True, stop=True)
-        nc.tensor.matmul(out=tabp[:, 0:DK], lhsT=ident[:], rhs=cos2[LAST], start=True, stop=True)
 
         zero_v(xs23)
         load_scales(xs23, x_scales, 256, 512)
@@ -281,6 +279,9 @@ def tile_multiheadedattention_pa_kernel(tc, x_words, x_scales, w_words, w_scales
                     for kk in (0, 1):
                         for g in gs:
                             mx_pass(0, kk, g, acc[kk], 0, NW)
+                    if gs == (0, 1):
+                        nc.tensor.matmul(out=tabp[:, DK : 2 * DK], lhsT=ident[:], rhs=sin2[LAST], start=True, stop=True)
+                        nc.tensor.matmul(out=tabp[:, 0:DK], lhsT=ident[:], rhs=cos2[LAST], start=True, stop=True)
             elif j > 1:
                 acc[j] = psum.tile([P, NW], F32, name="acc")
                 for g in range(G):

@@ -107,6 +107,7 @@ def tile_multiheadedattention_pa_kernel(tc, x_words, x_scales, w_words, w_scales
         zero_v(wss[0])
         cold = keep.tile([P, P + NW], BF16, name="cold")
         nc.vector.memset(cold[:], 0.0)
+        zero_v(xs23)
 
         pos = keep.tile([P, TB], F32, name="pos")
         nc.gpsimd.iota(pos[:], pattern=[[P, TB]], base=0, channel_multiplier=1, allow_small_or_imprecise_dtypes=True)
@@ -124,6 +125,8 @@ def tile_multiheadedattention_pa_kernel(tc, x_words, x_scales, w_words, w_scales
         load_codes(xc01b, x_words, 4, 8, 0, 512)
         load_codes(wc0c, w_words, 5, 8, 0, 2 * NW)
         nc.sync.dma_start(out=bias0[:], in_=b[0:NW].partition_broadcast(P))
+        load_scales(xs23, x_scales, 256, 512)
+        load_codes(xc23, x_words, 0, 8, 512, 1024)
 
         for i in range(WARM):
             dummy = psum.tile([P, NW], F32, name="acc")
@@ -188,9 +191,6 @@ def tile_multiheadedattention_pa_kernel(tc, x_words, x_scales, w_words, w_scales
         tables(LAST)
         tabp = tabs.tile([P, 2 * DK], F32, name="tabp")
 
-        zero_v(xs23)
-        load_scales(xs23, x_scales, 256, 512)
-        load_codes(xc23, x_words, 0, 8, 512, 1024)
         reduce_angles("a", 0, 2)
         zero_v(xs47)
         reduce_angles("b", 2, LAST)

@@ -79,13 +79,12 @@ def tile_multiheadedattention_pa_kernel(tc, x_words, x_scales, w_words, w_scales
                     in_=scales[:, 4 * q : 4 * q + 4, col0:col1].rearrange("g r n -> r g n").bitcast(I32),
                 )
 
-        xc01a = x_code_tile("xc01a", 0, 4, 0, 2)
-        xc01b = x_code_tile("xc01b", 4, 8, 0, 2)
-        xc23 = x_code_tile("xc23", 0, 8, 2, 4)
+        xc03a = x_code_tile("xc03a", 0, 2, 0, 4)
+        xc01b = x_code_tile("xc01b", 2, 8, 0, 2)
+        xc23b = x_code_tile("xc23b", 2, 8, 2, 4)
         xc47a = x_code_tile("xc47a", 0, 4, 4, 8)
         xc47b = x_code_tile("xc47b", 4, 8, 4, 8)
-        xs01 = x_plane_tile("xs01", 0, 2)
-        xs23 = x_plane_tile("xs23", 2, 4)
+        xs03 = x_plane_tile("xs03", 0, 4)
         xs47 = x_plane_tile("xs47", 4, 8)
         wc0a = w_code_tile("wc0a", 0, 0, 2)
         wc0b = w_code_tile("wc0b", 0, 2, 5)
@@ -103,11 +102,10 @@ def tile_multiheadedattention_pa_kernel(tc, x_words, x_scales, w_words, w_scales
 
         ones = keep.tile([P, 1], F32, name="ones")
         nc.vector.memset(ones[:], 1.0)
-        zero_v(xs01)
+        zero_v(xs03)
         zero_v(wss[0])
         cold = keep.tile([P, P + NW], BF16, name="cold")
         nc.vector.memset(cold[:], 0.0)
-        zero_v(xs23)
 
         pos = keep.tile([P, TB], F32, name="pos")
         nc.gpsimd.iota(pos[:], pattern=[[P, TB]], base=0, channel_multiplier=1, allow_small_or_imprecise_dtypes=True)
@@ -118,15 +116,14 @@ def tile_multiheadedattention_pa_kernel(tc, x_words, x_scales, w_words, w_scales
         nc.scalar.activation(out=junk[:], in_=ones[:], func=FUNC.Sin)
 
         load_codes(wc0a, w_words, 0, 2, 0, 2 * NW)
-        load_codes(xc01a, x_words, 0, 4, 0, 512)
-        load_scales(xs01, x_scales, 0, 256)
+        load_codes(xc03a, x_words, 0, 2, 0, 1024)
+        load_scales(xs03, x_scales, 0, 512)
         load_scales(wss[0], w_scales, 0, NW)
         load_codes(wc0b, w_words, 2, 5, 0, 2 * NW)
-        load_codes(xc01b, x_words, 4, 8, 0, 512)
+        load_codes(xc01b, x_words, 2, 8, 0, 512)
         load_codes(wc0c, w_words, 5, 8, 0, 2 * NW)
         nc.sync.dma_start(out=bias0[:], in_=b[0:NW].partition_broadcast(P))
-        load_scales(xs23, x_scales, 256, 512)
-        load_codes(xc23, x_words, 0, 8, 512, 1024)
+        load_codes(xc23b, x_words, 2, 8, 512, 1024)
 
         for i in range(WARM):
             dummy = psum.tile([P, NW], F32, name="acc")
@@ -273,16 +270,20 @@ def tile_multiheadedattention_pa_kernel(tc, x_words, x_scales, w_words, w_scales
         for j in range(n_main):
             nb, tb = order[j]
             if j == 0:
-                acc[0] = psum.tile([P, NW], F32, name="acc")
-                acc[1] = psum.tile([P, NW], F32, name="acc")
-                for gs in ((0, 1), (2, 3), (4,), (5, 6, 7)):
+                for kk in range(4):
+                    acc[kk] = psum.tile([P, NW], F32, name="acc")
+                    for g in (0, 1):
+                        mx_pass(0, kk, g, acc[kk], 0, NW)
+                nc.tensor.matmul(out=tabp[:, DK : 2 * DK], lhsT=ident[:], rhs=sin2[LAST], start=True, stop=True)
+                nc.tensor.matmul(out=tabp[:, 0:DK], lhsT=ident[:], rhs=cos2[LAST], start=True, stop=True)
+                for gs in ((2, 3), (4,), (5, 6, 7)):
                     for kk in (0, 1):
                         for g in gs:
                             mx_pass(0, kk, g, acc[kk], 0, NW)
-                    if gs == (0, 1):
-                        nc.tensor.matmul(out=tabp[:, DK : 2 * DK], lhsT=ident[:], rhs=sin2[LAST], start=True, stop=True)
-                        nc.tensor.matmul(out=tabp[:, 0:DK], lhsT=ident[:], rhs=cos2[LAST], start=True, stop=True)
-            elif j > 1:
+            elif j in (2, 3):
+                for g in range(2, G):
+                    mx_pass(nb, tb, g, acc[j], 0, NW)
+            elif j > 3:
                 acc[j] = psum.tile([P, NW], F32, name="acc")
                 for g in range(G):
                     mx_pass(nb, tb, g, acc[j], 0, NW)

@@ -22,7 +22,7 @@ FLOPS = 2 * 1024 * 4096 * 4096
 
 PI = 3.141592653589793
 G_COLS = 192
-WARM = 6
+WARM = 8
 
 
 def tile_multiheadedattention_pa_kernel(tc, x_words, x_scales, w_words, w_scales, b, out):
@@ -104,8 +104,6 @@ def tile_multiheadedattention_pa_kernel(tc, x_words, x_scales, w_words, w_scales
         nc.vector.memset(ones[:], 1.0)
         zero_v(xs03)
         zero_v(wss[0])
-        cold = keep.tile([P, P + NW], BF16, name="cold")
-        nc.vector.memset(cold[:], 0.0)
 
         pos = keep.tile([P, TB], F32, name="pos")
         nc.gpsimd.iota(pos[:], pattern=[[P, TB]], base=0, channel_multiplier=1, allow_small_or_imprecise_dtypes=True)
@@ -126,8 +124,8 @@ def tile_multiheadedattention_pa_kernel(tc, x_words, x_scales, w_words, w_scales
         load_codes(xc23b, x_words, 2, 8, 512, 1024)
 
         for i in range(WARM):
-            dummy = psum.tile([P, NW], F32, name="acc")
-            nc.tensor.matmul(out=dummy[:], lhsT=cold[:, 0:P], rhs=cold[:, P : P + NW], start=True, stop=True)
+            dummy = psum.tile([P, P], F32, name="acc")
+            nc.tensor.matmul(out=dummy[:], lhsT=ident[:], rhs=ident[:], start=True, stop=True)
 
         turns = keep.tile([P, HALF], F32, name="turns")
         for j in range(4):
@@ -185,8 +183,25 @@ def tile_multiheadedattention_pa_kernel(tc, x_words, x_scales, w_words, w_scales
 
         LAST = TB - 1
         reduce_angles("c", LAST, TB)
-        tables(LAST)
+        trig = keep.tile([P, 3, HALF], F32, name="trig")
+        nc.scalar.activation(out=trig[:, 0, :], in_=frac[LAST], func=FUNC.Sin, scale=2.0 * PI)
+        nc.scalar.activation(out=trig[:, 1, :], in_=frac[LAST], func=FUNC.Sin, scale=-2.0 * PI)
+        nc.scalar.activation(out=trig[:, 2, :], in_=size[LAST], func=FUNC.Sin, scale=-2.0 * PI, bias=halfpi[:, 0:1])
         tabp = tabs.tile([P, 2 * DK], F32, name="tabp")
+        nc.tensor.matmul(
+            out=tabp[:, DK : 2 * DK].rearrange("p (i e) -> p i e", e=2),
+            lhsT=ident[:],
+            rhs=trig[:, 0:2, :].rearrange("p e i -> p i e"),
+            start=True,
+            stop=True,
+        )
+        nc.tensor.matmul(
+            out=tabp[:, 0:DK].rearrange("p (i e) -> p i e", e=2),
+            lhsT=ident[:],
+            rhs=trig[:, 2, :].unsqueeze(2).to_broadcast([P, HALF, 2]),
+            start=True,
+            stop=True,
+        )
 
         reduce_angles("a", 0, 2)
         zero_v(xs47)
@@ -274,8 +289,6 @@ def tile_multiheadedattention_pa_kernel(tc, x_words, x_scales, w_words, w_scales
                     acc[kk] = psum.tile([P, NW], F32, name="acc")
                     for g in (0, 1):
                         mx_pass(0, kk, g, acc[kk], 0, NW)
-                nc.tensor.matmul(out=tabp[:, DK : 2 * DK], lhsT=ident[:], rhs=sin2[LAST], start=True, stop=True)
-                nc.tensor.matmul(out=tabp[:, 0:DK], lhsT=ident[:], rhs=cos2[LAST], start=True, stop=True)
                 for gs in ((2, 3), (4,), (5, 6, 7)):
                     for kk in (0, 1):
                         for g in gs:

@@ -22,7 +22,7 @@ FLOPS = 2 * 1024 * 4096 * 4096
 
 PI = 3.141592653589793
 G_COLS = 192
-WARM = 8
+WARM = 6
 
 
 def tile_multiheadedattention_pa_kernel(tc, x_words, x_scales, w_words, w_scales, b, out):
@@ -137,12 +137,24 @@ def tile_multiheadedattention_pa_kernel(tc, x_words, x_scales, w_words, w_scales
                 nc.vector.tensor_scalar(
                     out=turns[:, w * m : w * (m + 1)], in0=turns[:, 0:w], scalar1=10.0 ** (-w * m / 32.0), scalar2=None, op0=ALU.mult
                 )
+        LAST = TB - 1
+        turns_l = keep.tile([P, HALF], F32, name="turns_l")
+        whole_l = keep.tile([P, HALF], I32, name="whole_l")
+        frac_l = keep.tile([P, HALF], F32, name="frac_l")
+        size_l = keep.tile([P, HALF], F32, name="size_l")
+        for dst in (turns_l, whole_l):
+            nc.vector.tensor_scalar(out=dst[:, 0:64], in0=turns[:, 0:64], scalar1=pos[:, LAST:TB], scalar2=None, op0=ALU.mult)
+            nc.vector.tensor_scalar(
+                out=dst[:, 64:128], in0=turns[:, 0:64], scalar1=pos[:, LAST:TB], scalar2=10.0 ** (-2.0), op0=ALU.mult, op1=ALU.mult
+            )
         nc.vector.tensor_scalar(out=turns[:, 64:128], in0=turns[:, 0:64], scalar1=10.0 ** (-2.0), scalar2=None, op0=ALU.mult)
         halfpi = keep.tile([P, 1], F32, name="halfpi")
         nc.vector.tensor_scalar(out=halfpi[:], in0=ones[:], scalar1=PI / 2.0, scalar2=None, op0=ALU.mult)
+        nc.vector.tensor_tensor(out=frac_l[:], in0=turns_l[:], in1=whole_l[:], op=ALU.subtract)
+        nc.vector.scalar_tensor_tensor(out=size_l[:], in0=frac_l[:], scalar=-1.0, in1=frac_l[:], op0=ALU.mult, op1=ALU.max)
 
-        frac = {}
-        size = {}
+        frac = {LAST: frac_l[:]}
+        size = {LAST: size_l[:]}
 
         def reduce_angles(name, tb0, tb1):
             n = tb1 - tb0
@@ -181,8 +193,6 @@ def tile_multiheadedattention_pa_kernel(tc, x_words, x_scales, w_words, w_scales
             sin2[tb] = s
             both[tb] = cs
 
-        LAST = TB - 1
-        reduce_angles("c", LAST, TB)
         trig = keep.tile([P, 3, HALF], F32, name="trig")
         nc.scalar.activation(out=trig[:, 0, :], in_=frac[LAST], func=FUNC.Sin, scale=2.0 * PI)
         nc.scalar.activation(out=trig[:, 1, :], in_=frac[LAST], func=FUNC.Sin, scale=-2.0 * PI)

from contextlib import ExitStack

import concourse.mybir as mybir
from concourse.masks import make_identity

F32 = mybir.dt.float32
BF16 = mybir.dt.bfloat16
I32 = mybir.dt.int32
U8 = mybir.dt.uint8
FP4X4 = mybir.dt.float4_e2m1fn_x4
ALU = mybir.AluOpType
FUNC = mybir.ActivationFunctionType

P = 128
G = 8
TB = 8
NB = 8
NW = 512
DK = 256
HALF = DK // 2
FLOPS = 2 * 1024 * 4096 * 4096

PI = 3.141592653589793
G_COLS = 192
WARM = 6


def tile_multiheadedattention_pa_kernel(tc, x_words, x_scales, w_words, w_scales, b, out):
    nc = tc.nc
    with ExitStack() as ctx:
        keep = ctx.enter_context(tc.tile_pool(name="keep", bufs=1))
        work = ctx.enter_context(tc.tile_pool(name="work", bufs=3))
        outp = ctx.enter_context(tc.tile_pool(name="outp", bufs=6))
        psum = ctx.enter_context(tc.psum_pool(name="psum", bufs=7))
        tabs = ctx.enter_context(tc.psum_pool(name="tabs", bufs=1))
        ctx.enter_context(tc.manual_schedule())

        x_codes = {}
        x_scale = {}
        w_codes = {}
        w_scale = {}

        def x_code_tile(name, g0, g1, tb0, tb1):
            t = keep.tile([P, g1 - g0, 256 * (tb1 - tb0)], U8, name=name, align_bytes=256)
            for g in range(g0, g1):
                for tb in range(tb0, tb1):
                    x_codes[(tb, g)] = t[:, g - g0, 256 * (tb - tb0) : 256 * (tb - tb0 + 1)]
            return t

        def x_plane_tile(name, tb0, tb1):
            t = keep.tile([P, G, P * (tb1 - tb0)], U8, name=name, align_bytes=256)
            for g in range(G):
                for tb in range(tb0, tb1):
                    x_scale[(tb, g)] = t[:, g, P * (tb - tb0) : P * (tb - tb0 + 1)]
            return t

        def w_code_tile(name, nb, g0, g1):
            t = keep.tile([P, g1 - g0, 2 * NW], U8, name=name, align_bytes=256)
            for g in range(g0, g1):
                w_codes[(nb, g)] = t[:, g - g0, :]
            return t

        def w_plane_tile(name, nb):
            t = keep.tile([P, G, NW], U8, name=name, align_bytes=256)
            for g in range(G):
                w_scale[(nb, g)] = t[:, g, :]
            return t

        def load_codes(dst, words, g0, g1, byte0, byte1):
            nc.sync.dma_start(
                out=dst[:].bitcast(I32),
                in_=words[g0:g1, :, byte0:byte1].rearrange("g p n -> p g n").bitcast(I32),
            )

        def load_scales(dst, scales, col0, col1):
            for q in range(4):
                nc.sync.dma_start(
                    out=dst[32 * q : 32 * q + 4, :, :].bitcast(I32),
                    in_=scales[:, 4 * q : 4 * q + 4, col0:col1].rearrange("g r n -> r g n").bitcast(I32),
                )

        xc03a = x_code_tile("xc03a", 0, 2, 0, 4)
        xc01b = x_code_tile("xc01b", 2, 8, 0, 2)
        xc23b = x_code_tile("xc23b", 2, 8, 2, 4)
        xc47a = x_code_tile("xc47a", 0, 4, 4, 8)
        xc47b = x_code_tile("xc47b", 4, 8, 4, 8)
        xs03 = x_plane_tile("xs03", 0, 4)
        xs47 = x_plane_tile("xs47", 4, 8)
        wc0a = w_code_tile("wc0a", 0, 0, 2)
        wc0b = w_code_tile("wc0b", 0, 2, 5)
        wc0c = w_code_tile("wc0c", 0, 5, 8)
        wcs = [None] + [w_code_tile("wc%d" % nb, nb, 0, G) for nb in range(1, NB)]
        wss = [w_plane_tile("ws%d" % nb, nb) for nb in range(NB)]
        bias0 = keep.tile([P, NW], BF16, name="bias0")
        bias1 = keep.tile([P, (NB - 1) * NW], BF16, name="bias1")

        def zero_v(plane):
            nc.vector.memset(plane[:].bitcast(I32), 0)

        def zero_g(plane):
            nc.gpsimd.memset(plane[:].bitcast(F32), 0.0)

        ones = keep.tile([P, 1], F32, name="ones")
        nc.vector.memset(ones[:], 1.0)
        zero_v(xs03)
        zero_v(wss[0])

        pos = keep.tile([P, TB], F32, name="pos")
        nc.gpsimd.iota(pos[:], pattern=[[P, TB]], base=0, channel_multiplier=1, allow_small_or_imprecise_dtypes=True)
        ident = keep.tile([P, P], F32, name="ident")
        make_identity(nc, ident[:])

        junk = keep.tile([P, 1], F32, name="junk")
        nc.scalar.activation(out=junk[:], in_=ones[:], func=FUNC.Sin)

        load_codes(wc0a, w_words, 0, 2, 0, 2 * NW)
        load_codes(xc03a, x_words, 0, 2, 0, 1024)
        load_scales(xs03, x_scales, 0, 512)
        load_scales(wss[0], w_scales, 0, NW)
        load_codes(wc0b, w_words, 2, 5, 0, 2 * NW)
        load_codes(xc01b, x_words, 2, 8, 0, 512)
        load_codes(wc0c, w_words, 5, 8, 0, 2 * NW)
        nc.sync.dma_start(out=bias0[:], in_=b[0:NW].partition_broadcast(P))
        load_codes(xc23b, x_words, 2, 8, 512, 1024)

        for i in range(WARM):
            dummy = psum.tile([P, P], F32, name="acc")
            nc.tensor.matmul(out=dummy[:], lhsT=ident[:], rhs=ident[:], start=True, stop=True)

        turns = keep.tile([P, HALF], F32, name="turns")
        for j in range(4):
            nc.vector.tensor_scalar(
                out=turns[:, j : j + 1], in0=ones[:], scalar1=10.0 ** (-j / 32.0) / (2.0 * PI), scalar2=None, op0=ALU.mult
            )
        for w in (4, 16):
            for m in range(1, 4):
                nc.vector.tensor_scalar(
                    out=turns[:, w * m : w * (m + 1)], in0=turns[:, 0:w], scalar1=10.0 ** (-w * m / 32.0), scalar2=None, op0=ALU.mult
                )
        LAST = TB - 1
        turns_l = keep.tile([P, HALF], F32, name="turns_l")
        whole_l = keep.tile([P, HALF], I32, name="whole_l")
        frac_l = keep.tile([P, HALF], F32, name="frac_l")
        size_l = keep.tile([P, HALF], F32, name="size_l")
        for dst in (turns_l, whole_l):
            nc.vector.tensor_scalar(out=dst[:, 0:64], in0=turns[:, 0:64], scalar1=pos[:, LAST:TB], scalar2=None, op0=ALU.mult)
            nc.vector.tensor_scalar(
                out=dst[:, 64:128], in0=turns[:, 0:64], scalar1=pos[:, LAST:TB], scalar2=10.0 ** (-2.0), op0=ALU.mult, op1=ALU.mult
            )
        nc.vector.tensor_scalar(out=turns[:, 64:128], in0=turns[:, 0:64], scalar1=10.0 ** (-2.0), scalar2=None, op0=ALU.mult)
        halfpi = keep.tile([P, 1], F32, name="halfpi")
        nc.vector.tensor_scalar(out=halfpi[:], in0=ones[:], scalar1=PI / 2.0, scalar2=None, op0=ALU.mult)
        nc.vector.tensor_tensor(out=frac_l[:], in0=turns_l[:], in1=whole_l[:], op=ALU.subtract)
        nc.vector.scalar_tensor_tensor(out=size_l[:], in0=frac_l[:], scalar=-1.0, in1=frac_l[:], op0=ALU.mult, op1=ALU.max)

        frac = {LAST: frac_l[:]}
        size = {LAST: size_l[:]}

        def reduce_angles(name, tb0, tb1):
            n = tb1 - tb0
            u = keep.tile([P, n, HALF], F32, name="u" + name)
            k = keep.tile([P, n, HALF], I32, name="k" + name)
            d = keep.tile([P, n, HALF], F32, name="d" + name)
            a = keep.tile([P, n, HALF], F32, name="m" + name)
            for tb in range(tb0, tb1):
                nc.vector.tensor_scalar(out=u[:, tb - tb0, :], in0=turns[:], scalar1=pos[:, tb : tb + 1], scalar2=None, op0=ALU.mult)
            nc.vector.tensor_copy(out=k[:], in_=u[:])
            nc.vector.tensor_tensor(out=d[:], in0=u[:], in1=k[:], op=ALU.subtract)
            nc.vector.scalar_tensor_tensor(out=a[:], in0=d[:], scalar=-1.0, in1=d[:], op0=ALU.mult, op1=ALU.max)
            for tb in range(tb0, tb1):
                frac[tb] = d[:, tb - tb0, :]
                size[tb] = a[:, tb - tb0, :]

        cos2 = {}
        sin2 = {}
        both = {}

        def tables(tb):
            cs = keep.tile([P, 2 * DK], F32, name="cs%d" % tb)
            c = cs[:, 0:DK]
            s = cs[:, DK : 2 * DK]
            s3 = s.rearrange("p (i e) -> p i e", e=2)
            nc.scalar.activation(out=s3[:, :, 0], in_=frac[tb], func=FUNC.Sin, scale=2.0 * PI)
            nc.scalar.activation(out=s3[:, :, 1], in_=frac[tb], func=FUNC.Sin, scale=-2.0 * PI)
            nc.scalar.activation(
                out=c.rearrange("p (i e) -> p i e", e=2),
                in_=size[tb].unsqueeze(2).to_broadcast([P, HALF, 2]),
                func=FUNC.Sin,
                scale=-2.0 * PI,
                bias=halfpi[:, 0:1],
            )
            cos2[tb] = c
            sin2[tb] = s
            both[tb] = cs

        trig = keep.tile([P, 3, HALF], F32, name="trig")
        nc.scalar.activation(out=trig[:, 0, :], in_=frac[LAST], func=FUNC.Sin, scale=2.0 * PI)
        nc.scalar.activation(out=trig[:, 1, :], in_=frac[LAST], func=FUNC.Sin, scale=-2.0 * PI)
        nc.scalar.activation(out=trig[:, 2, :], in_=size[LAST], func=FUNC.Sin, scale=-2.0 * PI, bias=halfpi[:, 0:1])
        tabp = tabs.tile([P, 2 * DK], F32, name="tabp")
        nc.tensor.matmul(
            out=tabp[:, DK : 2 * DK].rearrange("p (i e) -> p i e", e=2),
            lhsT=ident[:],
            rhs=trig[:, 0:2, :].rearrange("p e i -> p i e"),
            start=True,
            stop=True,
        )
        nc.tensor.matmul(
            out=tabp[:, 0:DK].rearrange("p (i e) -> p i e", e=2),
            lhsT=ident[:],
            rhs=trig[:, 2, :].unsqueeze(2).to_broadcast([P, HALF, 2]),
            start=True,
            stop=True,
        )

        reduce_angles("a", 0, 2)
        zero_v(xs47)
        reduce_angles("b", 2, LAST)
        zero_v(wss[1])
        zero_v(wss[2])

        load_scales(xs47, x_scales, 512, 1024)
        load_codes(xc47a, x_words, 0, 4, 1024, 2048)
        load_codes(xc47b, x_words, 4, 8, 1024, 2048)
        load_scales(wss[1], w_scales, NW, 2 * NW)
        load_codes(wcs[1], w_words, 0, G, 2 * NW, 4 * NW)
        nc.sync.dma_start(out=bias1[:], in_=b[NW : NB * NW].partition_broadcast(P))
        load_scales(wss[2], w_scales, 2 * NW, 3 * NW)
        load_codes(wcs[2], w_words, 0, G, 4 * NW, 6 * NW)

        for tb in range(3):
            tables(tb)

        order = [(nb, tb) for nb in range(NB) for tb in range(LAST)]
        n_main = len(order)
        zt = {}
        tt = {}
        at = {}
        rt = {}
        ot = {}

        def mx_pass(nb, tb, g, sums, c0, c1):
            nc.tensor.matmul_mx(
                out=sums[:],
                lhsT=x_codes[(tb, g)].bitcast(FP4X4),
                lhsT_scale=x_scale[(tb, g)],
                rhs=w_codes[(nb, g)][:, 2 * c0 : 2 * c1].bitcast(FP4X4),
                rhs_scale=w_scale[(nb, g)][:, c0:c1],
                start=(g == 0),
                stop=(g == G - 1),
            )

        def by_head(ap):
            return ap.rearrange("p (h c) -> p h c", c=DK)

        def by_pair(ap):
            return ap.rearrange("p (i e) -> p i e", e=2)

        def bias_of(nb, c0, c1):
            return bias0[:, c0:c1] if nb == 0 else bias1[:, (nb - 1) * NW + c0 : (nb - 1) * NW + c1]

        def add_bias(k):
            zt[k] = work.tile([P, NW], F32, name="z")
            nc.vector.tensor_tensor(out=zt[k][:], in0=acc[k][:], in1=bias_of(order[k][0], 0, NW), op=ALU.add)

        def product(dst, k, table):
            nc.vector.tensor_tensor(
                out=by_head(dst[:]), in0=by_head(zt[k][:]), in1=table.unsqueeze(1).to_broadcast([P, 2, DK]), op=ALU.mult
            )

        def sine_product(k):
            tt[k] = work.tile([P, NW], F32, name="t")
            rt[k] = work.tile([P, NW], F32, name="r")
            product(tt[k], k, sin2[order[k][1]])
            nc.scalar.copy(out=by_pair(rt[k][:]), in_=by_pair(tt[k][:])[:, :, ::-1])

        def cosine_product(k):
            at[k] = work.tile([P, NW], F32, name="a")
            product(at[k], k, cos2[order[k][1]])

        def store(queue, o, nb, tb, c0, c1):
            queue.dma_start(
                out=out[0, 2 * nb + c0 // DK : 2 * nb + c1 // DK, P * tb : P * (tb + 1), :].rearrange("h p j -> p h j"),
                in_=by_head(o[:]),
            )

        def finish(k, g_cols, queue):
            o = outp.tile([P, NW], F32, name="o")
            nc.gpsimd.tensor_tensor(out=o[:, 0:g_cols], in0=at[k][:, 0:g_cols], in1=rt[k][:, 0:g_cols], op=ALU.add)
            if g_cols < NW:
                nc.vector.tensor_tensor(out=o[:, g_cols:NW], in0=at[k][:, g_cols:NW], in1=rt[k][:, g_cols:NW], op=ALU.add)
            store(queue, o, order[k][0], order[k][1], 0, NW)

        acc = {}
        for j in range(n_main):
            nb, tb = order[j]
            if j == 0:
                for kk in range(4):
                    acc[kk] = psum.tile([P, NW], F32, name="acc")
                    for g in (0, 1):
                        mx_pass(0, kk, g, acc[kk], 0, NW)
                for gs in ((2, 3), (4,), (5, 6, 7)):
                    for kk in (0, 1):
                        for g in gs:
                            mx_pass(0, kk, g, acc[kk], 0, NW)
            elif j in (2, 3):
                for g in range(2, G):
                    mx_pass(nb, tb, g, acc[j], 0, NW)
            elif j > 3:
                acc[j] = psum.tile([P, NW], F32, name="acc")
                for g in range(G):
                    mx_pass(nb, tb, g, acc[j], 0, NW)
            if j + 3 < LAST:
                tables(j + 3)
            add_bias(j)
            if j >= 2:
                finish(j - 2, G_COLS, nc.scalar)
            if 2 <= j <= NB - 2:
                nxt = j + 1
                zero_g(wss[nxt])
                load_scales(wss[nxt], w_scales, nxt * NW, (nxt + 1) * NW)
                load_codes(wcs[nxt], w_words, 0, G, 2 * nxt * NW, 2 * (nxt + 1) * NW)
            if j >= 1:
                cosine_product(j - 1)
            sine_product(j)

        def sums_of(nb, c0, c1):
            sums = psum.tile([P, c1 - c0], F32, name="acc")
            for g in range(G):
                mx_pass(nb, LAST, g, sums, c0, c1)
            return sums

        def biased(nb, c0, c1, sums):
            z = work.tile([P, c1 - c0], F32, name="z")
            nc.vector.tensor_tensor(out=z[:], in0=sums[:], in1=bias_of(nb, c0, c1), op=ALU.add)
            return z

        def both_products(z, wide):
            nh = wide // DK
            sc = work.tile([P, 2, wide], F32, name="sc")
            r = work.tile([P, wide], F32, name="r")
            nc.vector.tensor_tensor(
                out=sc[:].rearrange("p t (h c) -> p t h c", h=nh),
                in0=by_head(z[:]).unsqueeze(1).to_broadcast([P, 2, nh, DK]),
                in1=tabp[:].rearrange("p (t c) -> p t c", t=2).unsqueeze(2).to_broadcast([P, 2, nh, DK]),
                op=ALU.mult,
            )
            nc.scalar.copy(out=by_pair(r[:]), in_=by_pair(sc[:, 1, :])[:, :, ::-1])
            return sc, r

        def add_and_store(engine, queue, a, r, nb, c0, c1):
            o = outp.tile([P, c1 - c0], F32, name="o")
            engine.tensor_tensor(out=o[:], in0=a, in1=r[:], op=ALU.add)
            store(queue, o, nb, LAST, c0, c1)

        for nb in range(NB - 1):
            z = biased(nb, 0, NW, sums_of(nb, 0, NW))
            if nb == 0:
                finish(n_main - 2, G_COLS, nc.scalar)
                cosine_product(n_main - 1)
            sc, r = both_products(z, NW)
            if nb == 0:
                finish(n_main - 1, NW, nc.sync)
            add_and_store(nc.gpsimd, nc.sync, sc[:, 0, :], r, nb, 0, NW)

        nb = NB - 1
        sums0 = sums_of(nb, 0, DK)
        sums1 = sums_of(nb, DK, NW)
        z0 = biased(nb, 0, DK, sums0)
        z1 = biased(nb, DK, NW, sums1)
        sc0, r0 = both_products(z0, DK)
        a1 = work.tile([P, DK], F32, name="a")
        r1 = work.tile([P, DK], F32, name="r")
        nc.vector.tensor_tensor(out=a1[:], in0=z1[:], in1=tabp[:, 0:DK], op=ALU.mult)
        nc.vector.tensor_tensor(
            out=by_pair(r1[:]), in0=by_pair(z1[:])[:, :, ::-1], in1=by_pair(tabp[:, DK : 2 * DK])[:, :, ::-1], op=ALU.mult
        )
        add_and_store(nc.vector, nc.sync, sc0[:, 0, :], r0, nb, 0, DK)
        add_and_store(nc.vector, nc.scalar, a1[:], r1, nb, DK, NW)
